import numpy as np
import ml_dtypes


def mxq(x, axis, fmt="e4m3"):
    dtype, down = {"e4m3": (ml_dtypes.float8_e4m3fn, 7), "e5m2": (ml_dtypes.float8_e5m2, 14)}[fmt]
    v = np.moveaxis(np.asarray(x, np.float32).astype(ml_dtypes.bfloat16).astype(np.float64), axis, -1)
    blocks = v.reshape(v.shape[:-1] + (-1, 32))
    amax = np.abs(blocks).max(-1, keepdims=True)
    byte = np.maximum(np.where(amax > 0, np.frexp(amax)[1] - 1 + 127, 0) - down, 1)
    scale = np.exp2(byte - 127.0)
    codes = (blocks / scale).astype(np.float32).astype(dtype).astype(np.float64)
    return np.moveaxis((codes * scale).reshape(v.shape), -1, axis)


WIDE = False


def mx_kscale(k):
    if not WIDE:
        return np.ones(k)
    levels = np.array([10, -10, 5, -5, 0])
    a = np.random.permutation(np.resize(levels, k // 512 * 4)).reshape(k // 512, 4)
    idx = np.arange(k)
    return np.exp2(a[idx // 512, idx % 128 // 32])


BF16 = ml_dtypes.bfloat16


def bf(x):
    return np.asarray(x, np.float32).astype(BF16)


def f64(x):
    return np.asarray(x).astype(np.float64)


E2M1 = np.array([0.0, 0.5, 1.0, 1.5, 2.0, 3.0, 4.0, 6.0, -0.0, -0.5, -1.0, -1.5, -2.0, -3.0, -4.0, -6.0])


def pack_weight(w, fmt):
    k, n = w.shape
    w = f64(bf(w)).reshape(k // 32, 32, n)
    amax = np.abs(w).max(1)
    if fmt == "e4m3":
        byte = np.frexp(amax)[1] - 1 + 127 - 7
    else:
        mant, ex = np.frexp(amax / 6.0)
        byte = np.where(mant > 0.5, ex, ex - 1) + 127
    byte = np.clip(np.where(amax > 0, byte, 1), 1, 254)
    scaled = (w * np.exp2(127.0 - byte)[:, None, :]).reshape(k, n).astype(np.float32)
    by_word = np.ascontiguousarray(scaled.reshape(k // 512, 128, 4, n).transpose(0, 1, 3, 2))
    if fmt == "e4m3":
        words = by_word.astype(ml_dtypes.float8_e4m3fn).view(np.uint8)
    else:
        c = by_word.astype(ml_dtypes.float4_e2m1fn).view(np.uint8) & 0xF
        words = c[..., 0::2] | (c[..., 1::2] << 4)
    return np.ascontiguousarray(words), np.ascontiguousarray(byte.astype(np.uint8).reshape(k // 512, 16, n))


def unpack_weight(words, scales, fmt):
    g, p, n, _ = words.shape
    if fmt == "e4m3":
        vals = np.ascontiguousarray(words).view(ml_dtypes.float8_e4m3fn).astype(np.float64)
    else:
        nib = np.empty((g, p, n, 4), np.uint8)
        nib[..., 0::2] = words & 0xF
        nib[..., 1::2] = words >> 4
        vals = E2M1[nib]
    vals = vals * np.repeat(np.exp2(scales.astype(np.float64) - 127.0), 8, axis=1)[..., None]
    return vals.transpose(0, 1, 3, 2).reshape(g * 512, n)

def pack4(w):
    words, scales = pack_weight(w, "e2m1")
    return words.reshape(words.shape[0], 128, -1), scales


def unpack4(words, scales):
    return unpack_weight(words.reshape(words.shape[0], 128, -1, 2), scales, "e2m1")


B, C, T, E, H = 1, 512, 4, 1024, 8
D = E // H
S = C * T


def heads(y):
    return np.moveaxis(y.reshape(B, C, T, H, D), 3, 1)


def setup_inputs():
    s = mx_kscale(E)
    hidden_states = bf(np.random.standard_normal((B, S, E)) * s)
    wk_words, wk_scales = pack4((np.random.standard_normal((E, E)) * 2.0 / np.sqrt(E) / s[None, :]).T)
    bk = bf(np.random.standard_normal(E) * 0.3)
    wv_words, wv_scales = pack4((np.random.standard_normal((E, E)) * 2.0 / np.sqrt(E) / s[None, :]).T)
    bv = bf(np.random.standard_normal(E) * 0.3)
    return {"hidden_states": hidden_states,
            "wk_words": wk_words,
            "wk_scales": wk_scales,
            "bk": bk,
            "wv_words": wv_words,
            "wv_scales": wv_scales,
            "bv": bv}


def reference(hidden_states, wk_words, wk_scales, bk, wv_words, wv_scales, bv):
    xq = mxq(f64(hidden_states), 2, "e4m3")
    k = heads((xq @ unpack4(wk_words, wk_scales)) + f64(bk))
    v = heads((xq @ unpack4(wv_words, wv_scales)) + f64(bv))
    return k, v, k.mean(axis=3), v.mean(axis=3)

@@ -1,0 +1,203 @@
+import concourse.mybir as mybir
+from concourse.masks import make_identity
+
+F32 = mybir.dt.float32
+BF16 = mybir.dt.bfloat16
+I32 = mybir.dt.int32
+U32 = mybir.dt.uint32
+U8 = mybir.dt.uint8
+FP8X4 = mybir.dt.float8_e4m3fn_x4
+FP4X4 = mybir.dt.float4_e2m1fn_x4
+ADD = mybir.AluOpType.add
+
+P = 128
+TOKENS = 2048
+WIDTH = 1024
+PASSES = WIDTH // (4 * P)
+PAIRS = 2
+HEAD = 128
+HEADS = 2 * WIDTH // HEAD
+CHUNK = 4
+HALVES = 2
+CHUNKS = TOKENS // (HALVES * P * CHUNK)
+SLOTS = CHUNKS * CHUNK
+QUARTERS = HALVES * CHUNKS
+BANK = 512
+QUAD = BANK // HEAD
+QUADS = HEADS // QUAD
+GROUPS = HALVES * QUADS * CHUNKS
+VECTOR_MEANS_EVERY = 4
+
+FLOPS = 2 * TOKENS * WIDTH * 2 * WIDTH
+
+
+def tile_chunkedattention_pb_kernel(
+    tc, hidden_states, wk_words, wk_scales, bk, wv_words, wv_scales, bv, out_0, out_1, out_2, out_3
+):
+    nc = tc.nc
+    weights = [(wk_words, wk_scales, bk), (wv_words, wv_scales, bv)]
+    slots_in_hbm = hidden_states[0].rearrange("(a p j) e -> a j p e", a=HALVES, p=P)
+    heads_in_hbm = [
+        o[0].rearrange("h (a p i) t d -> a p h i t d", a=HALVES, p=P) for o in (out_0, out_1)
+    ]
+    means_in_hbm = [
+        o[0].rearrange("h (a p i) d -> a p h i d", a=HALVES, p=P) for o in (out_2, out_3)
+    ]
+
+    with tc.tile_pool(name="keep", bufs=1) as keep, tc.tile_pool(
+        name="regroup", bufs=4
+    ) as regroup, tc.tile_pool(name="results", bufs=6) as results, tc.tile_pool(
+        name="sums", bufs=3
+    ) as sums, tc.psum_pool(name="psum", bufs=8) as psum, tc.manual_schedule():
+        x_sb = keep.tile([P, HALVES, SLOTS, WIDTH], BF16)
+        x_codes = keep.tile([P, HALVES, SLOTS, PASSES, P], U32, align_bytes=64)
+        x_scales = keep.tile([P, HALVES, SLOTS, PASSES, P], U8, align_bytes=64)
+        w_codes = keep.tile([P, 2, PASSES, 2 * WIDTH], U8, align_bytes=64)
+        w_scales = keep.tile([P, 2, PASSES, WIDTH], U8, align_bytes=64)
+        bias_row = keep.tile([P, 2 * WIDTH], BF16)
+        bias_sb = keep.tile([P, HEADS, HEAD], F32)
+        ones = keep.tile([P, P], BF16)
+        identity = keep.tile([P, P], F32)
+
+        nc.vector.memset(bias_row[:], 0.0)
+        nc.vector.memset(w_scales[:].rearrange("p w g n -> p (w g n)").bitcast(I32), 0)
+        nc.vector.memset(ones[:], 1.0)
+        make_identity(nc, identity[:])
+
+        def load_quarter(quarter):
+            half, i = divmod(quarter, CHUNKS)
+            for j in range(i * CHUNK, (i + 1) * CHUNK):
+                nc.sync.dma_start(out=x_sb[:, half, j, :], in_=slots_in_hbm[half, j])
+
+        def load_weight(w):
+            words, scales, bias = weights[w]
+            nc.sync.dma_start(
+                out=w_codes[:, w, :, :].bitcast(I32),
+                in_=words.rearrange("g p b -> p g b").bitcast(I32),
+            )
+            for quadrant in range(4):
+                nc.sync.dma_start(
+                    out=w_scales[32 * quadrant : 32 * quadrant + 4, w, :, :].bitcast(I32),
+                    in_=scales[:, 4 * quadrant : 4 * quadrant + 4, :]
+                    .rearrange("g r n -> r g n")
+                    .bitcast(I32),
+                )
+            nc.scalar.dma_start(
+                out=bias_row[0:1, w * WIDTH : (w + 1) * WIDTH],
+                in_=bias.rearrange("(o n) -> o n", o=1),
+            )
+
+        load_quarter(0)
+        load_quarter(1)
+        load_weight(0)
+        load_quarter(2)
+        load_quarter(3)
+        load_weight(1)
+
+        def spread_biases():
+            bias_flat = bias_sb[:].rearrange("p h d -> p (h d)")
+            for c in range(0, 2 * WIDTH, BANK):
+                spread = psum.tile([P, BANK], F32, tag="bank")
+                nc.tensor.matmul(
+                    out=spread[:],
+                    lhsT=ones[:],
+                    rhs=bias_row[:, c : c + BANK],
+                    start=True,
+                    stop=True,
+                )
+                nc.scalar.copy(out=bias_flat[:, c : c + BANK], in_=spread[:])
+
+        def quantise_quarter(quarter):
+            half, i = divmod(quarter, CHUNKS)
+            for j in range(i * CHUNK, (i + 1) * CHUNK):
+                words = x_sb[:, half, j, :].bitcast(F32)
+                flipped = psum.tile([P, PASSES, PAIRS, P], F32, tag="bank")
+                for g in range(PASSES):
+                    for u in range(PAIRS):
+                        nc.tensor.transpose(
+                            out=flipped[:, g, u, :],
+                            in_=words[:, g * PAIRS * P + u : (g + 1) * PAIRS * P : PAIRS],
+                            identity=identity[:],
+                        )
+                grouped = regroup.tile([P, PASSES, P, 2 * PAIRS], BF16, align_bytes=64)
+                nc.scalar.copy(
+                    out=grouped[:]
+                    .rearrange("p g n t -> p (g n t)")
+                    .bitcast(F32)
+                    .rearrange("p (g n u) -> p g n u", g=PASSES, u=PAIRS),
+                    in_=flipped[:].rearrange("p g u n -> p g n u"),
+                )
+                nc.vector.quantize_mx(
+                    out=x_codes[:, half, j, :, :].rearrange("p g n -> p (g n)").bitcast(FP8X4),
+                    scales=x_scales[:, half, j, :, :].rearrange("p g n -> p (g n)"),
+                    in_=grouped[:].rearrange("p g n t -> p (g n t)"),
+                )
+
+        def place(group):
+            unit, i = divmod(group, CHUNKS)
+            half, quad = divmod(unit, QUADS)
+            w, quad_of_w = divmod(quad, QUADS // 2)
+            return half, w, quad_of_w * QUAD, i
+
+        def project(group):
+            half, w, h0, i = place(group)
+            y = results.tile([P, QUAD, CHUNK, HEAD], F32)
+            for t in range(CHUNK):
+                acc = psum.tile([P, QUAD, HEAD], F32, tag="bank")
+                for g in range(PASSES):
+                    nc.tensor.matmul_mx(
+                        out=acc[:].rearrange("p h d -> p (h d)"),
+                        lhsT=x_codes[:, half, i * CHUNK + t, g, :].bitcast(FP8X4),
+                        lhsT_scale=x_scales[:, half, i * CHUNK + t, g, :],
+                        rhs=w_codes[:, w, g, 2 * HEAD * h0 : 2 * HEAD * (h0 + QUAD)].bitcast(FP4X4),
+                        rhs_scale=w_scales[:, w, g, HEAD * h0 : HEAD * (h0 + QUAD)],
+                        start=(g == 0),
+                        stop=(g == PASSES - 1),
+                    )
+                first = w * (HEADS // 2) + h0
+                nc.vector.tensor_tensor(
+                    out=y[:, :, t, :], in0=acc[:], in1=bias_sb[:, first : first + QUAD, :], op=ADD
+                )
+            nc.sync.dma_start(out=heads_in_hbm[w][half, :, h0 : h0 + QUAD, i], in_=y[:])
+            return y
+
+        means_of_unit = {}
+
+        def chunk_means(group, y):
+            half, w, h0, i = place(group)
+            total = sums.tile([P, QUAD, HEAD], F32)
+            if group % VECTOR_MEANS_EVERY == VECTOR_MEANS_EVERY - 1:
+                nc.vector.tensor_reduce(
+                    out=total[:],
+                    in_=y[:].rearrange("p h t d -> p h d t"),
+                    axis=mybir.AxisListType.X,
+                    op=ADD,
+                )
+            else:
+                pairs = sums.tile([P, QUAD, CHUNK // 2, HEAD], F32)
+                nc.gpsimd.tensor_tensor(
+                    out=pairs[:], in0=y[:, :, 0:CHUNK:2, :], in1=y[:, :, 1:CHUNK:2, :], op=ADD
+                )
+                nc.gpsimd.tensor_tensor(
+                    out=total[:], in0=pairs[:, :, 0, :], in1=pairs[:, :, 1, :], op=ADD
+                )
+            if i == 0:
+                mean = sums.tile([P, QUAD, CHUNKS, HEAD], F32)
+                means_of_unit[group // CHUNKS] = mean
+            mean = means_of_unit[group // CHUNKS]
+            nc.scalar.mul(out=mean[:, :, i, :], in_=total[:], mul=1.0 / CHUNK)
+            if i == CHUNKS - 1:
+                nc.scalar.dma_start(out=means_in_hbm[w][half, :, h0 : h0 + QUAD], in_=mean[:])
+
+        for quarter in range(CHUNKS):
+            quantise_quarter(quarter)
+        spread_biases()
+        waiting = None
+        for group in range(GROUPS):
+            if CHUNKS <= group < QUARTERS:
+                quantise_quarter(group)
+            y = project(group)
+            if waiting is not None:
+                chunk_means(group - 1, waiting)
+            waiting = y
+        chunk_means(GROUPS - 1, waiting)

@@ -109,8 +109,9 @@ def tile_chunkedattention_pb_kernel(
 
         def quantise_quarter(quarter):
             half, i = divmod(quarter, CHUNKS)
-            for j in range(i * CHUNK, (i + 1) * CHUNK):
-                words = x_sb[:, half, j, :].bitcast(F32)
+            grouped = regroup.tile([P, CHUNK, PASSES, P, 2 * PAIRS], BF16, align_bytes=64)
+            for t in range(CHUNK):
+                words = x_sb[:, half, i * CHUNK + t, :].bitcast(F32)
                 flipped = psum.tile([P, PASSES, PAIRS, P], F32, tag="bank")
                 for g in range(PASSES):
                     for u in range(PAIRS):
@@ -119,19 +120,19 @@ def tile_chunkedattention_pb_kernel(
                             in_=words[:, g * PAIRS * P + u : (g + 1) * PAIRS * P : PAIRS],
                             identity=identity[:],
                         )
-                grouped = regroup.tile([P, PASSES, P, 2 * PAIRS], BF16, align_bytes=64)
                 nc.scalar.copy(
-                    out=grouped[:]
+                    out=grouped[:, t]
                     .rearrange("p g n t -> p (g n t)")
                     .bitcast(F32)
                     .rearrange("p (g n u) -> p g n u", g=PASSES, u=PAIRS),
                     in_=flipped[:].rearrange("p g u n -> p g n u"),
                 )
-                nc.vector.quantize_mx(
-                    out=x_codes[:, half, j, :, :].rearrange("p g n -> p (g n)").bitcast(FP8X4),
-                    scales=x_scales[:, half, j, :, :].rearrange("p g n -> p (g n)"),
-                    in_=grouped[:].rearrange("p g n t -> p (g n t)"),
-                )
+            slots = slice(i * CHUNK, (i + 1) * CHUNK)
+            nc.vector.quantize_mx(
+                out=x_codes[:, half, slots, :, :].rearrange("p j g n -> p (j g n)").bitcast(FP8X4),
+                scales=x_scales[:, half, slots, :, :].rearrange("p j g n -> p (j g n)"),
+                in_=grouped[:].rearrange("p j g n t -> p (j g n t)"),
+            )
 
         def place(group):
             unit, i = divmod(group, CHUNKS)

@@ -27,6 +27,8 @@ QUAD = BANK // HEAD
 QUADS = HEADS // QUAD
 GROUPS = HALVES * QUADS * CHUNKS
 VECTOR_MEANS_EVERY = 4
+LATE_QUARTERS_BEFORE = (4, 6)
+SCALE_LAG = 2
 
 FLOPS = 2 * TOKENS * WIDTH * 2 * WIDTH
 
@@ -47,8 +49,10 @@ def tile_chunkedattention_pb_kernel(
     with tc.tile_pool(name="keep", bufs=1) as keep, tc.tile_pool(
         name="regroup", bufs=4
     ) as regroup, tc.tile_pool(name="results", bufs=6) as results, tc.tile_pool(
-        name="sums", bufs=3
-    ) as sums, tc.psum_pool(name="psum", bufs=8) as psum, tc.manual_schedule():
+        name="sums", bufs=6
+    ) as sums, tc.tile_pool(name="halfway", bufs=2) as halfway, tc.tile_pool(
+        name="means", bufs=3
+    ) as means, tc.psum_pool(name="psum", bufs=8) as psum, tc.manual_schedule():
         x_sb = keep.tile([P, HALVES, SLOTS, WIDTH], BF16)
         x_codes = keep.tile([P, HALVES, SLOTS, PASSES, P], U32, align_bytes=64)
         x_scales = keep.tile([P, HALVES, SLOTS, PASSES, P], U8, align_bytes=64)
@@ -163,9 +167,10 @@ def tile_chunkedattention_pb_kernel(
             return y
 
         means_of_unit = {}
+        totals = {}
+        projected = {}
 
-        def chunk_means(group, y):
-            half, w, h0, i = place(group)
+        def chunk_sums(group, y):
             total = sums.tile([P, QUAD, HEAD], F32)
             if group % VECTOR_MEANS_EVERY == VECTOR_MEANS_EVERY - 1:
                 nc.vector.tensor_reduce(
@@ -175,30 +180,34 @@ def tile_chunkedattention_pb_kernel(
                     op=ADD,
                 )
             else:
-                pairs = sums.tile([P, QUAD, CHUNK // 2, HEAD], F32)
+                pairs = halfway.tile([P, QUAD, CHUNK // 2, HEAD], F32)
                 nc.gpsimd.tensor_tensor(
                     out=pairs[:], in0=y[:, :, 0:CHUNK:2, :], in1=y[:, :, 1:CHUNK:2, :], op=ADD
                 )
                 nc.gpsimd.tensor_tensor(
                     out=total[:], in0=pairs[:, :, 0, :], in1=pairs[:, :, 1, :], op=ADD
                 )
+            totals[group] = total
+
+        def chunk_means(group):
+            half, w, h0, i = place(group)
             if i == 0:
-                mean = sums.tile([P, QUAD, CHUNKS, HEAD], F32)
+                mean = means.tile([P, QUAD, CHUNKS, HEAD], F32)
                 means_of_unit[group // CHUNKS] = mean
             mean = means_of_unit[group // CHUNKS]
-            nc.scalar.mul(out=mean[:, :, i, :], in_=total[:], mul=1.0 / CHUNK)
+            nc.scalar.mul(out=mean[:, :, i, :], in_=totals[group][:], mul=1.0 / CHUNK)
             if i == CHUNKS - 1:
                 nc.scalar.dma_start(out=means_in_hbm[w][half, :, h0 : h0 + QUAD], in_=mean[:])
 
         for quarter in range(CHUNKS):
             quantise_quarter(quarter)
         spread_biases()
-        waiting = None
-        for group in range(GROUPS):
-            if CHUNKS <= group < QUARTERS:
-                quantise_quarter(group)
-            y = project(group)
-            if waiting is not None:
-                chunk_means(group - 1, waiting)
-            waiting = y
-        chunk_means(GROUPS - 1, waiting)
+        for step in range(GROUPS + 1 + SCALE_LAG):
+            if step in LATE_QUARTERS_BEFORE:
+                quantise_quarter(CHUNKS + LATE_QUARTERS_BEFORE.index(step))
+            if step < GROUPS:
+                projected[step] = project(step)
+            if 0 <= step - 1 < GROUPS:
+                chunk_sums(step - 1, projected[step - 1])
+            if 0 <= step - 1 - SCALE_LAG:
+                chunk_means(step - 1 - SCALE_LAG)

@@ -23,9 +23,8 @@ CHUNKS = TOKENS // (HALVES * P * CHUNK)
 SLOTS = CHUNKS * CHUNK
 QUARTERS = HALVES * CHUNKS
 BANK = 512
-QUAD = BANK // HEAD
-QUADS = HEADS // QUAD
-GROUPS = HALVES * QUADS * CHUNKS
+PAIR = 2
+GROUPS = HALVES * HEADS // PAIR
 VECTOR_MEANS_EVERY = 4
 LATE_QUARTERS_BEFORE = (4, 6)
 SCALE_LAG = 2
@@ -139,31 +138,38 @@ def tile_chunkedattention_pb_kernel(
             )
 
         def place(group):
-            unit, i = divmod(group, CHUNKS)
-            half, quad = divmod(unit, QUADS)
-            w, quad_of_w = divmod(quad, QUADS // 2)
-            return half, w, quad_of_w * QUAD, i
+            half, pair = divmod(group, HEADS // PAIR)
+            w, pair_of_w = divmod(pair, HEADS // (2 * PAIR))
+            return half, w, pair_of_w * PAIR
 
         def project(group):
-            half, w, h0, i = place(group)
-            y = results.tile([P, QUAD, CHUNK, HEAD], F32)
-            for t in range(CHUNK):
-                acc = psum.tile([P, QUAD, HEAD], F32, tag="bank")
-                for g in range(PASSES):
-                    nc.tensor.matmul_mx(
-                        out=acc[:].rearrange("p h d -> p (h d)"),
-                        lhsT=x_codes[:, half, i * CHUNK + t, g, :].bitcast(FP8X4),
-                        lhsT_scale=x_scales[:, half, i * CHUNK + t, g, :],
-                        rhs=w_codes[:, w, g, 2 * HEAD * h0 : 2 * HEAD * (h0 + QUAD)].bitcast(FP4X4),
-                        rhs_scale=w_scales[:, w, g, HEAD * h0 : HEAD * (h0 + QUAD)],
-                        start=(g == 0),
-                        stop=(g == PASSES - 1),
+            half, w, h0 = place(group)
+            y = results.tile([P, PAIR, CHUNKS, CHUNK, HEAD], F32)
+            for hh in range(PAIR):
+                head = h0 + hh
+                bias_of_head = bias_sb[:, w * (HEADS // 2) + head, :].unsqueeze(1)
+                for i in range(CHUNKS):
+                    acc = psum.tile([P, CHUNK, HEAD], F32, tag="bank")
+                    for t in range(CHUNK):
+                        for g in range(PASSES):
+                            nc.tensor.matmul_mx(
+                                out=acc[:, t, :],
+                                lhsT=x_codes[:, half, i * CHUNK + t, g, :].bitcast(FP8X4),
+                                lhsT_scale=x_scales[:, half, i * CHUNK + t, g, :],
+                                rhs=w_codes[:, w, g, 2 * HEAD * head : 2 * HEAD * (head + 1)].bitcast(
+                                    FP4X4
+                                ),
+                                rhs_scale=w_scales[:, w, g, HEAD * head : HEAD * (head + 1)],
+                                start=(g == 0),
+                                stop=(g == PASSES - 1),
+                            )
+                    nc.vector.tensor_tensor(
+                        out=y[:, hh, i],
+                        in0=acc[:],
+                        in1=bias_of_head.to_broadcast([P, CHUNK, HEAD]),
+                        op=ADD,
                     )
-                first = w * (HEADS // 2) + h0
-                nc.vector.tensor_tensor(
-                    out=y[:, :, t, :], in0=acc[:], in1=bias_sb[:, first : first + QUAD, :], op=ADD
-                )
-            nc.sync.dma_start(out=heads_in_hbm[w][half, :, h0 : h0 + QUAD, i], in_=y[:])
+            nc.sync.dma_start(out=heads_in_hbm[w][half, :, h0 : h0 + PAIR], in_=y[:])
             return y
 
         means_of_unit = {}
@@ -171,18 +177,19 @@ def tile_chunkedattention_pb_kernel(
         projected = {}
 
         def chunk_sums(group, y):
-            total = sums.tile([P, QUAD, HEAD], F32)
+            total = sums.tile([P, PAIR * CHUNKS, HEAD], F32)
+            chunks = y[:].rearrange("p h i t d -> p (h i) t d")
             if group % VECTOR_MEANS_EVERY == VECTOR_MEANS_EVERY - 1:
                 nc.vector.tensor_reduce(
                     out=total[:],
-                    in_=y[:].rearrange("p h t d -> p h d t"),
+                    in_=chunks.rearrange("p c t d -> p c d t"),
                     axis=mybir.AxisListType.X,
                     op=ADD,
                 )
             else:
-                pairs = halfway.tile([P, QUAD, CHUNK // 2, HEAD], F32)
+                pairs = halfway.tile([P, PAIR * CHUNKS, CHUNK // 2, HEAD], F32)
                 nc.gpsimd.tensor_tensor(
-                    out=pairs[:], in0=y[:, :, 0:CHUNK:2, :], in1=y[:, :, 1:CHUNK:2, :], op=ADD
+                    out=pairs[:], in0=chunks[:, :, 0:CHUNK:2, :], in1=chunks[:, :, 1:CHUNK:2, :], op=ADD
                 )
                 nc.gpsimd.tensor_tensor(
                     out=total[:], in0=pairs[:, :, 0, :], in1=pairs[:, :, 1, :], op=ADD
@@ -190,14 +197,21 @@ def tile_chunkedattention_pb_kernel(
             totals[group] = total
 
         def chunk_means(group):
-            half, w, h0, i = place(group)
-            if i == 0:
-                mean = means.tile([P, QUAD, CHUNKS, HEAD], F32)
-                means_of_unit[group // CHUNKS] = mean
-            mean = means_of_unit[group // CHUNKS]
-            nc.scalar.mul(out=mean[:, :, i, :], in_=totals[group][:], mul=1.0 / CHUNK)
-            if i == CHUNKS - 1:
-                nc.scalar.dma_start(out=means_in_hbm[w][half, :, h0 : h0 + QUAD], in_=mean[:])
+            half, w, h0 = place(group)
+            second = group % 2
+            if not second:
+                mean = means.tile([P, 2 * PAIR, CHUNKS, HEAD], F32)
+                means_of_unit[group // 2] = mean
+            mean = means_of_unit[group // 2]
+            nc.scalar.mul(
+                out=mean[:, second * PAIR : (second + 1) * PAIR].rearrange("p h i d -> p (h i) d"),
+                in_=totals[group][:],
+                mul=1.0 / CHUNK,
+            )
+            if second:
+                nc.scalar.dma_start(
+                    out=means_in_hbm[w][half, :, h0 - PAIR : h0 + PAIR], in_=mean[:]
+                )
 
         for quarter in range(CHUNKS):
             quantise_quarter(quarter)

@@ -25,7 +25,7 @@ QUARTERS = HALVES * CHUNKS
 BANK = 512
 PAIR = 2
 GROUPS = HALVES * HEADS // PAIR
-VECTOR_MEANS_EVERY = 4
+VECTOR_SUMS = (2, 10, 13, 15)
 LATE_QUARTERS_BEFORE = (4, 6)
 SCALE_LAG = 2
 
@@ -179,7 +179,7 @@ def tile_chunkedattention_pb_kernel(
         def chunk_sums(group, y):
             total = sums.tile([P, PAIR * CHUNKS, HEAD], F32)
             chunks = y[:].rearrange("p h i t d -> p (h i) t d")
-            if group % VECTOR_MEANS_EVERY == VECTOR_MEANS_EVERY - 1:
+            if group in VECTOR_SUMS:
                 nc.vector.tensor_reduce(
                     out=total[:],
                     in_=chunks.rearrange("p c t d -> p c d t"),

@@ -25,7 +25,8 @@ QUARTERS = HALVES * CHUNKS
 BANK = 512
 PAIR = 2
 GROUPS = HALVES * HEADS // PAIR
-VECTOR_SUMS = (2, 10, 13, 15)
+VECTOR_SUMS = (2, 10, 15)
+TENSOR_SUMS = (13, 14)
 LATE_QUARTERS_BEFORE = (4, 6)
 SCALE_LAG = 2
 
@@ -51,7 +52,9 @@ def tile_chunkedattention_pb_kernel(
         name="sums", bufs=6
     ) as sums, tc.tile_pool(name="halfway", bufs=2) as halfway, tc.tile_pool(
         name="means", bufs=3
-    ) as means, tc.psum_pool(name="psum", bufs=8) as psum, tc.manual_schedule():
+    ) as means, tc.tile_pool(name="turn", bufs=2) as turn, tc.psum_pool(
+        name="psum", bufs=8
+    ) as psum, tc.manual_schedule():
         x_sb = keep.tile([P, HALVES, SLOTS, WIDTH], BF16)
         x_codes = keep.tile([P, HALVES, SLOTS, PASSES, P], U32, align_bytes=64)
         x_scales = keep.tile([P, HALVES, SLOTS, PASSES, P], U8, align_bytes=64)
@@ -196,6 +199,33 @@ def tile_chunkedattention_pb_kernel(
                 )
             totals[group] = total
 
+        quartered_of = {}
+
+        def add_up_transposed(group, y):
+            chunks = y[:].rearrange("p h i t d -> p (h i) t d")
+            upright = psum.tile([P, PAIR * CHUNKS, P], F32, tag="bank")
+            for c in range(PAIR * CHUNKS):
+                for t in range(CHUNK):
+                    nc.tensor.matmul(
+                        out=upright[:, c, :],
+                        lhsT=chunks[:, c, t, :],
+                        rhs=identity[:],
+                        is_transpose=True,
+                        start=(t == 0),
+                        stop=(t == CHUNK - 1),
+                    )
+            quartered = turn.tile([P, PAIR * CHUNKS, P], F32)
+            nc.scalar.mul(out=quartered[:], in_=upright[:], mul=1.0 / CHUNK)
+            quartered_of[group] = quartered
+
+        def turn_means_back(group):
+            back = psum.tile([P, PAIR * CHUNKS, HEAD], F32, tag="bank")
+            for c in range(PAIR * CHUNKS):
+                nc.tensor.transpose(
+                    out=back[:, c, :], in_=quartered_of[group][:, c, :], identity=identity[:]
+                )
+            totals[group] = back
+
         def chunk_means(group):
             half, w, h0 = place(group)
             second = group % 2
@@ -203,11 +233,11 @@ def tile_chunkedattention_pb_kernel(
                 mean = means.tile([P, 2 * PAIR, CHUNKS, HEAD], F32)
                 means_of_unit[group // 2] = mean
             mean = means_of_unit[group // 2]
-            nc.scalar.mul(
-                out=mean[:, second * PAIR : (second + 1) * PAIR].rearrange("p h i d -> p (h i) d"),
-                in_=totals[group][:],
-                mul=1.0 / CHUNK,
-            )
+            share = mean[:, second * PAIR : (second + 1) * PAIR].rearrange("p h i d -> p (h i) d")
+            if group in TENSOR_SUMS:
+                nc.scalar.copy(out=share, in_=totals[group][:])
+            else:
+                nc.scalar.mul(out=share, in_=totals[group][:], mul=1.0 / CHUNK)
             if second:
                 nc.scalar.dma_start(
                     out=means_in_hbm[w][half, :, h0 - PAIR : h0 + PAIR], in_=mean[:]
@@ -221,7 +251,12 @@ def tile_chunkedattention_pb_kernel(
                 quantise_quarter(CHUNKS + LATE_QUARTERS_BEFORE.index(step))
             if step < GROUPS:
                 projected[step] = project(step)
-            if 0 <= step - 1 < GROUPS:
+            if step == GROUPS - 1:
+                for group in TENSOR_SUMS:
+                    add_up_transposed(group, projected[group])
+                for group in TENSOR_SUMS:
+                    turn_means_back(group)
+            if 0 <= step - 1 < GROUPS and step - 1 not in TENSOR_SUMS:
                 chunk_sums(step - 1, projected[step - 1])
             if 0 <= step - 1 - SCALE_LAG:
                 chunk_means(step - 1 - SCALE_LAG)

@@ -23,11 +23,14 @@ CHUNKS = TOKENS // (HALVES * P * CHUNK)
 SLOTS = CHUNKS * CHUNK
 QUARTERS = HALVES * CHUNKS
 BANK = 512
+BLOCK = 4
+BLOCKS = WIDTH // (BLOCK * HEAD)
 PAIR = 2
-GROUPS = HALVES * HEADS // PAIR
+BANKS = 4
 VECTOR_SUMS = (2, 10, 15)
 TENSOR_SUMS = (13, 14)
-LATE_QUARTERS_BEFORE = (4, 6)
+TURN_BEFORE = {4: (2, 0), 5: (2, 1), 6: (3, 0), 7: (3, 1)}
+QUANTISE_BEFORE = {6: 2, 8: 3}
 SCALE_LAG = 2
 
 FLOPS = 2 * TOKENS * WIDTH * 2 * WIDTH
@@ -48,10 +51,10 @@ def tile_chunkedattention_pb_kernel(
 
     with tc.tile_pool(name="keep", bufs=1) as keep, tc.tile_pool(
         name="regroup", bufs=4
-    ) as regroup, tc.tile_pool(name="results", bufs=6) as results, tc.tile_pool(
+    ) as regroup, tc.tile_pool(name="results", bufs=4) as results, tc.tile_pool(
         name="sums", bufs=6
     ) as sums, tc.tile_pool(name="halfway", bufs=2) as halfway, tc.tile_pool(
-        name="means", bufs=3
+        name="means", bufs=4
     ) as means, tc.tile_pool(name="turn", bufs=2) as turn, tc.psum_pool(
         name="psum", bufs=8
     ) as psum, tc.manual_schedule():
@@ -63,12 +66,14 @@ def tile_chunkedattention_pb_kernel(
         bias_row = keep.tile([P, 2 * WIDTH], BF16)
         bias_sb = keep.tile([P, HEADS, HEAD], F32)
         ones = keep.tile([P, P], BF16)
+        table_loader = keep.tile([P, 1], BF16)
         identity = keep.tile([P, P], F32)
 
-        nc.vector.memset(bias_row[:], 0.0)
-        nc.vector.memset(w_scales[:].rearrange("p w g n -> p (w g n)").bitcast(I32), 0)
         nc.vector.memset(ones[:], 1.0)
+        nc.vector.memset(w_scales[:].rearrange("p w g n -> p (w g n)").bitcast(I32), 0)
         make_identity(nc, identity[:])
+        nc.gpsimd.memset(bias_row[:].bitcast(I32), 0)
+        nc.scalar.copy(out=table_loader[:], in_=ones[:, 0:1])
 
         def load_quarter(quarter):
             half, i = divmod(quarter, CHUNKS)
@@ -88,7 +93,7 @@ def tile_chunkedattention_pb_kernel(
                     .rearrange("g r n -> r g n")
                     .bitcast(I32),
                 )
-            nc.scalar.dma_start(
+            nc.gpsimd.dma_start(
                 out=bias_row[0:1, w * WIDTH : (w + 1) * WIDTH],
                 in_=bias.rearrange("(o n) -> o n", o=1),
             )
@@ -100,9 +105,9 @@ def tile_chunkedattention_pb_kernel(
         load_quarter(3)
         load_weight(1)
 
-        def spread_biases():
+        def spread_bias(w):
             bias_flat = bias_sb[:].rearrange("p h d -> p (h d)")
-            for c in range(0, 2 * WIDTH, BANK):
+            for c in range(w * WIDTH, (w + 1) * WIDTH, BANK):
                 spread = psum.tile([P, BANK], F32, tag="bank")
                 nc.tensor.matmul(
                     out=spread[:],
@@ -113,10 +118,14 @@ def tile_chunkedattention_pb_kernel(
                 )
                 nc.scalar.copy(out=bias_flat[:, c : c + BANK], in_=spread[:])
 
-        def quantise_quarter(quarter):
+        grouped_of = {}
+
+        def transpose_slots(quarter, slots):
             half, i = divmod(quarter, CHUNKS)
-            grouped = regroup.tile([P, CHUNK, PASSES, P, 2 * PAIRS], BF16, align_bytes=64)
-            for t in range(CHUNK):
+            if quarter not in grouped_of:
+                grouped = regroup.tile([P, CHUNK, PASSES, P, 2 * PAIRS], BF16, align_bytes=64)
+                grouped_of[quarter] = grouped
+            for t in slots:
                 words = x_sb[:, half, i * CHUNK + t, :].bitcast(F32)
                 flipped = psum.tile([P, PASSES, PAIRS, P], F32, tag="bank")
                 for g in range(PASSES):
@@ -126,62 +135,96 @@ def tile_chunkedattention_pb_kernel(
                             in_=words[:, g * PAIRS * P + u : (g + 1) * PAIRS * P : PAIRS],
                             identity=identity[:],
                         )
-                nc.scalar.copy(
-                    out=grouped[:, t]
+                side_by_side = (
+                    grouped_of[quarter][:, t]
                     .rearrange("p g n t -> p (g n t)")
                     .bitcast(F32)
-                    .rearrange("p (g n u) -> p g n u", g=PASSES, u=PAIRS),
-                    in_=flipped[:].rearrange("p g u n -> p g n u"),
+                    .rearrange("p (g n u) -> p g n u", g=PASSES, u=PAIRS)
                 )
+                pairs = flipped[:].rearrange("p g u n -> p g n u")
+                if half == 0 and t % 2:
+                    nc.vector.tensor_copy(out=side_by_side, in_=pairs)
+                else:
+                    nc.scalar.copy(out=side_by_side, in_=pairs)
+
+        def quantise_quarter(quarter):
+            half, i = divmod(quarter, CHUNKS)
             slots = slice(i * CHUNK, (i + 1) * CHUNK)
             nc.vector.quantize_mx(
                 out=x_codes[:, half, slots, :, :].rearrange("p j g n -> p (j g n)").bitcast(FP8X4),
                 scales=x_scales[:, half, slots, :, :].rearrange("p j g n -> p (j g n)"),
-                in_=grouped[:].rearrange("p j g n t -> p (j g n t)"),
+                in_=grouped_of[quarter][:].rearrange("p j g n t -> p (j g n t)"),
             )
 
-        def place(group):
-            half, pair = divmod(group, HEADS // PAIR)
-            w, pair_of_w = divmod(pair, HEADS // (2 * PAIR))
-            return half, w, pair_of_w * PAIR
+        units = [(half, w, block) for half in range(HALVES) for w in range(2) for block in range(BLOCKS)]
+        groups = [(unit, part) for unit in units for part in range(2)]
+        results_of = {}
+        means_of = {}
+        totals = {}
+        quartered_of = {}
+
+        def products(acc, half, slot, w, h0, heads):
+            for g in range(PASSES):
+                nc.tensor.matmul_mx(
+                    out=acc,
+                    lhsT=x_codes[:, half, slot, g, :].bitcast(FP8X4),
+                    lhsT_scale=x_scales[:, half, slot, g, :],
+                    rhs=w_codes[:, w, g, 2 * HEAD * h0 : 2 * HEAD * (h0 + heads)].bitcast(FP4X4),
+                    rhs_scale=w_scales[:, w, g, HEAD * h0 : HEAD * (h0 + heads)],
+                    start=(g == 0),
+                    stop=(g == PASSES - 1),
+                )
+
+        def chunks_of(group):
+            unit, part = groups[group]
+            y = results_of[unit]
+            if unit == units[-1]:
+                return y[:, part * PAIR : (part + 1) * PAIR].rearrange("p h i t d -> p (h i) t d")
+            return y[:, :, part]
 
         def project(group):
-            half, w, h0 = place(group)
-            y = results.tile([P, PAIR, CHUNKS, CHUNK, HEAD], F32)
-            for hh in range(PAIR):
-                head = h0 + hh
-                bias_of_head = bias_sb[:, w * (HEADS // 2) + head, :].unsqueeze(1)
-                for i in range(CHUNKS):
-                    acc = psum.tile([P, CHUNK, HEAD], F32, tag="bank")
-                    for t in range(CHUNK):
-                        for g in range(PASSES):
-                            nc.tensor.matmul_mx(
-                                out=acc[:, t, :],
-                                lhsT=x_codes[:, half, i * CHUNK + t, g, :].bitcast(FP8X4),
-                                lhsT_scale=x_scales[:, half, i * CHUNK + t, g, :],
-                                rhs=w_codes[:, w, g, 2 * HEAD * head : 2 * HEAD * (head + 1)].bitcast(
-                                    FP4X4
-                                ),
-                                rhs_scale=w_scales[:, w, g, HEAD * head : HEAD * (head + 1)],
-                                start=(g == 0),
-                                stop=(g == PASSES - 1),
-                            )
+            unit, part = groups[group]
+            half, w, block = unit
+            h0 = block * BLOCK
+            if unit not in results_of:
+                y = results.tile([P, BLOCK, CHUNKS, CHUNK, HEAD], F32)
+                results_of[unit] = y
+            y = results_of[unit]
+            first_bias = w * (HEADS // 2) + h0
+            if unit != units[-1]:
+                for t in range(CHUNK):
+                    acc = psum.tile([P, BLOCK * HEAD], F32, tag="bank")
+                    products(acc[:], half, part * CHUNK + t, w, h0, BLOCK)
                     nc.vector.tensor_tensor(
-                        out=y[:, hh, i],
-                        in0=acc[:],
-                        in1=bias_of_head.to_broadcast([P, CHUNK, HEAD]),
+                        out=y[:, :, part, t, :],
+                        in0=acc[:].rearrange("p (h d) -> p h d", d=HEAD),
+                        in1=bias_sb[:, first_bias : first_bias + BLOCK, :],
                         op=ADD,
                     )
-            nc.sync.dma_start(out=heads_in_hbm[w][half, :, h0 : h0 + PAIR], in_=y[:])
-            return y
+                if part == 1:
+                    nc.sync.dma_start(out=heads_in_hbm[w][half, :, h0 : h0 + BLOCK], in_=y[:])
+            else:
+                heads = slice(part * PAIR, (part + 1) * PAIR)
+                for h in range(BLOCK)[heads]:
+                    bias_of_head = bias_sb[:, first_bias + h, :].unsqueeze(1)
+                    for i in range(CHUNKS):
+                        acc = psum.tile([P, CHUNK, HEAD], F32, tag="bank")
+                        for t in range(CHUNK):
+                            products(acc[:, t, :], half, i * CHUNK + t, w, h0 + h, 1)
+                        nc.vector.tensor_tensor(
+                            out=y[:, h, i],
+                            in0=acc[:],
+                            in1=bias_of_head.to_broadcast([P, CHUNK, HEAD]),
+                            op=ADD,
+                        )
+                nc.sync.dma_start(
+                    out=heads_in_hbm[w][half, :, h0 + part * PAIR : h0 + (part + 1) * PAIR],
+                    in_=y[:, heads],
+                )
 
-        means_of_unit = {}
-        totals = {}
-        projected = {}
-
-        def chunk_sums(group, y):
-            total = sums.tile([P, PAIR * CHUNKS, HEAD], F32)
-            chunks = y[:].rearrange("p h i t d -> p (h i) t d")
+        def chunk_sums(group):
+            total = sums.tile([P, BANKS, HEAD], F32)
+            chunks = chunks_of(group)
             if group in VECTOR_SUMS:
                 nc.vector.tensor_reduce(
                     out=total[:],
@@ -190,7 +233,7 @@ def tile_chunkedattention_pb_kernel(
                     op=ADD,
                 )
             else:
-                pairs = halfway.tile([P, PAIR * CHUNKS, CHUNK // 2, HEAD], F32)
+                pairs = halfway.tile([P, BANKS, CHUNK // 2, HEAD], F32)
                 nc.gpsimd.tensor_tensor(
                     out=pairs[:], in0=chunks[:, :, 0:CHUNK:2, :], in1=chunks[:, :, 1:CHUNK:2, :], op=ADD
                 )
@@ -199,12 +242,10 @@ def tile_chunkedattention_pb_kernel(
                 )
             totals[group] = total
 
-        quartered_of = {}
-
-        def add_up_transposed(group, y):
-            chunks = y[:].rearrange("p h i t d -> p (h i) t d")
-            upright = psum.tile([P, PAIR * CHUNKS, P], F32, tag="bank")
-            for c in range(PAIR * CHUNKS):
+        def add_up_transposed(group):
+            chunks = chunks_of(group)
+            upright = psum.tile([P, BANKS, P], F32, tag="bank")
+            for c in range(BANKS):
                 for t in range(CHUNK):
                     nc.tensor.matmul(
                         out=upright[:, c, :],
@@ -214,49 +255,58 @@ def tile_chunkedattention_pb_kernel(
                         start=(t == 0),
                         stop=(t == CHUNK - 1),
                     )
-            quartered = turn.tile([P, PAIR * CHUNKS, P], F32)
+            quartered = turn.tile([P, BANKS, P], F32)
             nc.scalar.mul(out=quartered[:], in_=upright[:], mul=1.0 / CHUNK)
             quartered_of[group] = quartered
 
         def turn_means_back(group):
-            back = psum.tile([P, PAIR * CHUNKS, HEAD], F32, tag="bank")
-            for c in range(PAIR * CHUNKS):
+            back = psum.tile([P, BANKS, HEAD], F32, tag="bank")
+            for c in range(BANKS):
                 nc.tensor.transpose(
                     out=back[:, c, :], in_=quartered_of[group][:, c, :], identity=identity[:]
                 )
             totals[group] = back
 
         def chunk_means(group):
-            half, w, h0 = place(group)
-            second = group % 2
-            if not second:
-                mean = means.tile([P, 2 * PAIR, CHUNKS, HEAD], F32)
-                means_of_unit[group // 2] = mean
-            mean = means_of_unit[group // 2]
-            share = mean[:, second * PAIR : (second + 1) * PAIR].rearrange("p h i d -> p (h i) d")
+            unit, part = groups[group]
+            half, w, block = unit
+            if unit not in means_of:
+                mean = means.tile([P, BLOCK, CHUNKS, HEAD], F32)
+                means_of[unit] = mean
+            mean = means_of[unit]
+            if unit == units[-1]:
+                share = mean[:, part * PAIR : (part + 1) * PAIR].rearrange("p h i d -> p (h i) d")
+            else:
+                share = mean[:, :, part, :]
             if group in TENSOR_SUMS:
                 nc.scalar.copy(out=share, in_=totals[group][:])
             else:
                 nc.scalar.mul(out=share, in_=totals[group][:], mul=1.0 / CHUNK)
-            if second:
+            if part == 1:
                 nc.scalar.dma_start(
-                    out=means_in_hbm[w][half, :, h0 - PAIR : h0 + PAIR], in_=mean[:]
+                    out=means_in_hbm[w][half, :, block * BLOCK : (block + 1) * BLOCK], in_=mean[:]
                 )
 
         for quarter in range(CHUNKS):
+            transpose_slots(quarter, range(CHUNK))
             quantise_quarter(quarter)
-        spread_biases()
-        for step in range(GROUPS + 1 + SCALE_LAG):
-            if step in LATE_QUARTERS_BEFORE:
-                quantise_quarter(CHUNKS + LATE_QUARTERS_BEFORE.index(step))
-            if step < GROUPS:
-                projected[step] = project(step)
-            if step == GROUPS - 1:
+        spread_bias(0)
+        for step in range(len(groups) + 1 + SCALE_LAG):
+            if step in TURN_BEFORE:
+                quarter, part = TURN_BEFORE[step]
+                transpose_slots(quarter, range(part * CHUNK // 2, (part + 1) * CHUNK // 2))
+            if step in QUANTISE_BEFORE:
+                quantise_quarter(QUANTISE_BEFORE[step])
+            if step == 1:
+                spread_bias(1)
+            if step < len(groups):
+                project(step)
+            if step == len(groups) - 1:
                 for group in TENSOR_SUMS:
-                    add_up_transposed(group, projected[group])
+                    add_up_transposed(group)
                 for group in TENSOR_SUMS:
                     turn_means_back(group)
-            if 0 <= step - 1 < GROUPS and step - 1 not in TENSOR_SUMS:
-                chunk_sums(step - 1, projected[step - 1])
+            if 0 <= step - 1 < len(groups) and step - 1 not in TENSOR_SUMS:
+                chunk_sums(step - 1)
             if 0 <= step - 1 - SCALE_LAG:
                 chunk_means(step - 1 - SCALE_LAG)

@@ -41,7 +41,7 @@ def tile_chunkedattention_pb_kernel(
 ):
     nc = tc.nc
     weights = [(wk_words, wk_scales, bk), (wv_words, wv_scales, bv)]
-    slots_in_hbm = hidden_states[0].rearrange("(a p j) e -> a j p e", a=HALVES, p=P)
+    slots_in_hbm = hidden_states[0].rearrange("(a p j) e -> a p j e", a=HALVES, p=P)
     heads_in_hbm = [
         o[0].rearrange("h (a p i) t d -> a p h i t d", a=HALVES, p=P) for o in (out_0, out_1)
     ]
@@ -75,10 +75,12 @@ def tile_chunkedattention_pb_kernel(
         nc.gpsimd.memset(bias_row[:].bitcast(I32), 0)
         nc.scalar.copy(out=table_loader[:], in_=ones[:, 0:1])
 
-        def load_quarter(quarter):
+        def load_quarter(quarter, slots):
             half, i = divmod(quarter, CHUNKS)
-            for j in range(i * CHUNK, (i + 1) * CHUNK):
-                nc.sync.dma_start(out=x_sb[:, half, j, :], in_=slots_in_hbm[half, j])
+            for j in range(i * CHUNK, (i + 1) * CHUNK, slots):
+                nc.sync.dma_start(
+                    out=x_sb[:, half, j : j + slots, :], in_=slots_in_hbm[half, :, j : j + slots, :]
+                )
 
         def load_weight(w):
             words, scales, bias = weights[w]
@@ -98,11 +100,11 @@ def tile_chunkedattention_pb_kernel(
                 in_=bias.rearrange("(o n) -> o n", o=1),
             )
 
-        load_quarter(0)
-        load_quarter(1)
+        load_quarter(0, 1)
+        load_quarter(1, 2)
         load_weight(0)
-        load_quarter(2)
-        load_quarter(3)
+        load_quarter(2, CHUNK)
+        load_quarter(3, CHUNK)
         load_weight(1)
 
         def spread_bias(w):
@@ -201,7 +203,11 @@ def tile_chunkedattention_pb_kernel(
                         in1=bias_sb[:, first_bias : first_bias + BLOCK, :],
                         op=ADD,
                     )
-                if part == 1:
+                if unit == units[0]:
+                    nc.sync.dma_start(
+                        out=heads_in_hbm[w][half, :, h0 : h0 + BLOCK, part], in_=y[:, :, part]
+                    )
+                elif part == 1:
                     nc.sync.dma_start(out=heads_in_hbm[w][half, :, h0 : h0 + BLOCK], in_=y[:])
             else:
                 heads = slice(part * PAIR, (part + 1) * PAIR)

import concourse.mybir as mybir
from concourse.masks import make_identity

F32 = mybir.dt.float32
BF16 = mybir.dt.bfloat16
I32 = mybir.dt.int32
U32 = mybir.dt.uint32
U8 = mybir.dt.uint8
FP8X4 = mybir.dt.float8_e4m3fn_x4
FP4X4 = mybir.dt.float4_e2m1fn_x4
ADD = mybir.AluOpType.add

P = 128
TOKENS = 2048
WIDTH = 1024
PASSES = WIDTH // (4 * P)
PAIRS = 2
HEAD = 128
HEADS = 2 * WIDTH // HEAD
CHUNK = 4
HALVES = 2
CHUNKS = TOKENS // (HALVES * P * CHUNK)
SLOTS = CHUNKS * CHUNK
QUARTERS = HALVES * CHUNKS
BANK = 512
BLOCK = 4
BLOCKS = WIDTH // (BLOCK * HEAD)
PAIR = 2
BANKS = 4
VECTOR_SUMS = (2, 10, 15)
TENSOR_SUMS = (13, 14)
TURN_BEFORE = {4: (2, 0), 5: (2, 1), 6: (3, 0), 7: (3, 1)}
QUANTISE_BEFORE = {6: 2, 8: 3}
SCALE_LAG = 2

FLOPS = 2 * TOKENS * WIDTH * 2 * WIDTH


def tile_chunkedattention_pb_kernel(
    tc, hidden_states, wk_words, wk_scales, bk, wv_words, wv_scales, bv, out_0, out_1, out_2, out_3
):
    nc = tc.nc
    weights = [(wk_words, wk_scales, bk), (wv_words, wv_scales, bv)]
    slots_in_hbm = hidden_states[0].rearrange("(a p j) e -> a p j e", a=HALVES, p=P)
    heads_in_hbm = [
        o[0].rearrange("h (a p i) t d -> a p h i t d", a=HALVES, p=P) for o in (out_0, out_1)
    ]
    means_in_hbm = [
        o[0].rearrange("h (a p i) d -> a p h i d", a=HALVES, p=P) for o in (out_2, out_3)
    ]

    with tc.tile_pool(name="keep", bufs=1) as keep, tc.tile_pool(
        name="regroup", bufs=4
    ) as regroup, tc.tile_pool(name="results", bufs=4) as results, tc.tile_pool(
        name="sums", bufs=6
    ) as sums, tc.tile_pool(name="halfway", bufs=2) as halfway, tc.tile_pool(
        name="means", bufs=4
    ) as means, tc.tile_pool(name="turn", bufs=2) as turn, tc.psum_pool(
        name="psum", bufs=8
    ) as psum, tc.manual_schedule():
        x_sb = keep.tile([P, HALVES, SLOTS, WIDTH], BF16)
        x_codes = keep.tile([P, HALVES, SLOTS, PASSES, P], U32, align_bytes=64)
        x_scales = keep.tile([P, HALVES, SLOTS, PASSES, P], U8, align_bytes=64)
        w_codes = keep.tile([P, 2, PASSES, 2 * WIDTH], U8, align_bytes=64)
        w_scales = keep.tile([P, 2, PASSES, WIDTH], U8, align_bytes=64)
        bias_row = keep.tile([P, 2 * WIDTH], BF16)
        bias_sb = keep.tile([P, HEADS, HEAD], F32)
        ones = keep.tile([P, P], BF16)
        table_loader = keep.tile([P, 1], BF16)
        identity = keep.tile([P, P], F32)

        nc.vector.memset(ones[:], 1.0)
        nc.vector.memset(w_scales[:].rearrange("p w g n -> p (w g n)").bitcast(I32), 0)
        make_identity(nc, identity[:])
        nc.gpsimd.memset(bias_row[:].bitcast(I32), 0)
        nc.scalar.copy(out=table_loader[:], in_=ones[:, 0:1])

        def load_quarter(quarter, slots):
            half, i = divmod(quarter, CHUNKS)
            for j in range(i * CHUNK, (i + 1) * CHUNK, slots):
                nc.sync.dma_start(
                    out=x_sb[:, half, j : j + slots, :], in_=slots_in_hbm[half, :, j : j + slots, :]
                )

        def load_weight(w):
            words, scales, bias = weights[w]
            nc.sync.dma_start(
                out=w_codes[:, w, :, :].bitcast(I32),
                in_=words.rearrange("g p b -> p g b").bitcast(I32),
            )
            for quadrant in range(4):
                nc.sync.dma_start(
                    out=w_scales[32 * quadrant : 32 * quadrant + 4, w, :, :].bitcast(I32),
                    in_=scales[:, 4 * quadrant : 4 * quadrant + 4, :]
                    .rearrange("g r n -> r g n")
                    .bitcast(I32),
                )
            nc.gpsimd.dma_start(
                out=bias_row[0:1, w * WIDTH : (w + 1) * WIDTH],
                in_=bias.rearrange("(o n) -> o n", o=1),
            )

        load_quarter(0, 1)
        load_quarter(1, 2)
        load_weight(0)
        load_quarter(2, CHUNK)
        load_quarter(3, CHUNK)
        load_weight(1)

        def spread_bias(w):
            bias_flat = bias_sb[:].rearrange("p h d -> p (h d)")
            for c in range(w * WIDTH, (w + 1) * WIDTH, BANK):
                spread = psum.tile([P, BANK], F32, tag="bank")
                nc.tensor.matmul(
                    out=spread[:],
                    lhsT=ones[:],
                    rhs=bias_row[:, c : c + BANK],
                    start=True,
                    stop=True,
                )
                nc.scalar.copy(out=bias_flat[:, c : c + BANK], in_=spread[:])

        grouped_of = {}

        def transpose_slots(quarter, slots):
            half, i = divmod(quarter, CHUNKS)
            if quarter not in grouped_of:
                grouped = regroup.tile([P, CHUNK, PASSES, P, 2 * PAIRS], BF16, align_bytes=64)
                grouped_of[quarter] = grouped
            for t in slots:
                words = x_sb[:, half, i * CHUNK + t, :].bitcast(F32)
                flipped = psum.tile([P, PASSES, PAIRS, P], F32, tag="bank")
                for g in range(PASSES):
                    for u in range(PAIRS):
                        nc.tensor.transpose(
                            out=flipped[:, g, u, :],
                            in_=words[:, g * PAIRS * P + u : (g + 1) * PAIRS * P : PAIRS],
                            identity=identity[:],
                        )
                side_by_side = (
                    grouped_of[quarter][:, t]
                    .rearrange("p g n t -> p (g n t)")
                    .bitcast(F32)
                    .rearrange("p (g n u) -> p g n u", g=PASSES, u=PAIRS)
                )
                pairs = flipped[:].rearrange("p g u n -> p g n u")
                if half == 0 and t % 2:
                    nc.vector.tensor_copy(out=side_by_side, in_=pairs)
                else:
                    nc.scalar.copy(out=side_by_side, in_=pairs)

        def quantise_quarter(quarter):
            half, i = divmod(quarter, CHUNKS)
            slots = slice(i * CHUNK, (i + 1) * CHUNK)
            nc.vector.quantize_mx(
                out=x_codes[:, half, slots, :, :].rearrange("p j g n -> p (j g n)").bitcast(FP8X4),
                scales=x_scales[:, half, slots, :, :].rearrange("p j g n -> p (j g n)"),
                in_=grouped_of[quarter][:].rearrange("p j g n t -> p (j g n t)"),
            )

        units = [(half, w, block) for half in range(HALVES) for w in range(2) for block in range(BLOCKS)]
        groups = [(unit, part) for unit in units for part in range(2)]
        results_of = {}
        means_of = {}
        totals = {}
        quartered_of = {}

        def products(acc, half, slot, w, h0, heads):
            for g in range(PASSES):
                nc.tensor.matmul_mx(
                    out=acc,
                    lhsT=x_codes[:, half, slot, g, :].bitcast(FP8X4),
                    lhsT_scale=x_scales[:, half, slot, g, :],
                    rhs=w_codes[:, w, g, 2 * HEAD * h0 : 2 * HEAD * (h0 + heads)].bitcast(FP4X4),
                    rhs_scale=w_scales[:, w, g, HEAD * h0 : HEAD * (h0 + heads)],
                    start=(g == 0),
                    stop=(g == PASSES - 1),
                )

        def chunks_of(group):
            unit, part = groups[group]
            y = results_of[unit]
            if unit == units[-1]:
                return y[:, part * PAIR : (part + 1) * PAIR].rearrange("p h i t d -> p (h i) t d")
            return y[:, :, part]

        def project(group):
            unit, part = groups[group]
            half, w, block = unit
            h0 = block * BLOCK
            if unit not in results_of:
                y = results.tile([P, BLOCK, CHUNKS, CHUNK, HEAD], F32)
                results_of[unit] = y
            y = results_of[unit]
            first_bias = w * (HEADS // 2) + h0
            if unit != units[-1]:
                for t in range(CHUNK):
                    acc = psum.tile([P, BLOCK * HEAD], F32, tag="bank")
                    products(acc[:], half, part * CHUNK + t, w, h0, BLOCK)
                    nc.vector.tensor_tensor(
                        out=y[:, :, part, t, :],
                        in0=acc[:].rearrange("p (h d) -> p h d", d=HEAD),
                        in1=bias_sb[:, first_bias : first_bias + BLOCK, :],
                        op=ADD,
                    )
                if unit == units[0]:
                    nc.sync.dma_start(
                        out=heads_in_hbm[w][half, :, h0 : h0 + BLOCK, part], in_=y[:, :, part]
                    )
                elif part == 1:
                    nc.sync.dma_start(out=heads_in_hbm[w][half, :, h0 : h0 + BLOCK], in_=y[:])
            else:
                heads = slice(part * PAIR, (part + 1) * PAIR)
                for h in range(BLOCK)[heads]:
                    bias_of_head = bias_sb[:, first_bias + h, :].unsqueeze(1)
                    for i in range(CHUNKS):
                        acc = psum.tile([P, CHUNK, HEAD], F32, tag="bank")
                        for t in range(CHUNK):
                            products(acc[:, t, :], half, i * CHUNK + t, w, h0 + h, 1)
                        nc.vector.tensor_tensor(
                            out=y[:, h, i],
                            in0=acc[:],
                            in1=bias_of_head.to_broadcast([P, CHUNK, HEAD]),
                            op=ADD,
                        )
                nc.sync.dma_start(
                    out=heads_in_hbm[w][half, :, h0 + part * PAIR : h0 + (part + 1) * PAIR],
                    in_=y[:, heads],
                )

        def chunk_sums(group):
            total = sums.tile([P, BANKS, HEAD], F32)
            chunks = chunks_of(group)
            if group in VECTOR_SUMS:
                nc.vector.tensor_reduce(
                    out=total[:],
                    in_=chunks.rearrange("p c t d -> p c d t"),
                    axis=mybir.AxisListType.X,
                    op=ADD,
                )
            else:
                pairs = halfway.tile([P, BANKS, CHUNK // 2, HEAD], F32)
                nc.gpsimd.tensor_tensor(
                    out=pairs[:], in0=chunks[:, :, 0:CHUNK:2, :], in1=chunks[:, :, 1:CHUNK:2, :], op=ADD
                )
                nc.gpsimd.tensor_tensor(
                    out=total[:], in0=pairs[:, :, 0, :], in1=pairs[:, :, 1, :], op=ADD
                )
            totals[group] = total

        def add_up_transposed(group):
            chunks = chunks_of(group)
            upright = psum.tile([P, BANKS, P], F32, tag="bank")
            for c in range(BANKS):
                for t in range(CHUNK):
                    nc.tensor.matmul(
                        out=upright[:, c, :],
                        lhsT=chunks[:, c, t, :],
                        rhs=identity[:],
                        is_transpose=True,
                        start=(t == 0),
                        stop=(t == CHUNK - 1),
                    )
            quartered = turn.tile([P, BANKS, P], F32)
            nc.scalar.mul(out=quartered[:], in_=upright[:], mul=1.0 / CHUNK)
            quartered_of[group] = quartered

        def turn_means_back(group):
            back = psum.tile([P, BANKS, HEAD], F32, tag="bank")
            for c in range(BANKS):
                nc.tensor.transpose(
                    out=back[:, c, :], in_=quartered_of[group][:, c, :], identity=identity[:]
                )
            totals[group] = back

        def chunk_means(group):
            unit, part = groups[group]
            half, w, block = unit
            if unit not in means_of:
                mean = means.tile([P, BLOCK, CHUNKS, HEAD], F32)
                means_of[unit] = mean
            mean = means_of[unit]
            if unit == units[-1]:
                share = mean[:, part * PAIR : (part + 1) * PAIR].rearrange("p h i d -> p (h i) d")
            else:
                share = mean[:, :, part, :]
            if group in TENSOR_SUMS:
                nc.scalar.copy(out=share, in_=totals[group][:])
            else:
                nc.scalar.mul(out=share, in_=totals[group][:], mul=1.0 / CHUNK)
            if part == 1:
                nc.scalar.dma_start(
                    out=means_in_hbm[w][half, :, block * BLOCK : (block + 1) * BLOCK], in_=mean[:]
                )

        for quarter in range(CHUNKS):
            transpose_slots(quarter, range(CHUNK))
            quantise_quarter(quarter)
        spread_bias(0)
        for step in range(len(groups) + 1 + SCALE_LAG):
            if step in TURN_BEFORE:
                quarter, part = TURN_BEFORE[step]
                transpose_slots(quarter, range(part * CHUNK // 2, (part + 1) * CHUNK // 2))
            if step in QUANTISE_BEFORE:
                quantise_quarter(QUANTISE_BEFORE[step])
            if step == 1:
                spread_bias(1)
            if step < len(groups):
                project(step)
            if step == len(groups) - 1:
                for group in TENSOR_SUMS:
                    add_up_transposed(group)
                for group in TENSOR_SUMS:
                    turn_means_back(group)
            if 0 <= step - 1 < len(groups) and step - 1 not in TENSOR_SUMS:
                chunk_sums(step - 1)
            if 0 <= step - 1 - SCALE_LAG:
                chunk_means(step - 1 - SCALE_LAG)
